import numpy as np
import ml_dtypes


def mxq(x, axis, fmt="e4m3"):
    dtype, down = {"e4m3": (ml_dtypes.float8_e4m3fn, 7), "e5m2": (ml_dtypes.float8_e5m2, 14)}[fmt]
    v = np.moveaxis(np.asarray(x, np.float32).astype(ml_dtypes.bfloat16).astype(np.float64), axis, -1)
    blocks = v.reshape(v.shape[:-1] + (-1, 32))
    amax = np.abs(blocks).max(-1, keepdims=True)
    byte = np.maximum(np.where(amax > 0, np.frexp(amax)[1] - 1 + 127, 0) - down, 1)
    scale = np.exp2(byte - 127.0)
    codes = (blocks / scale).astype(np.float32).astype(dtype).astype(np.float64)
    return np.moveaxis((codes * scale).reshape(v.shape), -1, axis)


WIDE = False


def mx_kscale(k):
    if not WIDE:
        return np.ones(k)
    levels = np.array([10, -10, 5, -5, 0])
    a = np.random.permutation(np.resize(levels, k // 512 * 4)).reshape(k // 512, 4)
    idx = np.arange(k)
    return np.exp2(a[idx // 512, idx % 128 // 32])


BF16 = ml_dtypes.bfloat16


def bf(x):
    return np.asarray(x, np.float32).astype(BF16)


def f64(x):
    return np.asarray(x).astype(np.float64)


B, T, E, H, DC, KB, DFF = 2, 1024, 1024, 16, 2, 512, 4096
HD = E // H
HALF = H // 2


def mix_matrices(mix_w, decay):
    i = np.arange(T)[:, None]
    j = np.arange(T)[None, :]
    d = np.clip(decay, 0.9, 1.0)
    expo = (j - i) / DC
    dec = d[:, None, None] ** expo
    causal = j >= i
    mcol = np.where(causal, mix_w[:HALF, None, :] * dec[:HALF], 0.0)
    mrow = np.where(causal, mix_w[HALF:, :, None] * dec[HALF:], 0.0)
    return np.concatenate([mcol, mrow], axis=0)


def setup_inputs():
    s = mx_kscale(T)
    u = mx_kscale(E)[::HD]
    st = np.concatenate([np.ones((HALF, T)), np.tile(s, (HALF, 1))], axis=0)
    return {"p": bf(np.random.standard_normal((B, H, T, HD)) / st[None, :, :, None]),
            "mix_w": bf(np.random.standard_normal((H, T)) * 3.0 / np.sqrt(T) * st * u[:, None]),
            "mix_b": bf(np.random.standard_normal((H, T)) * 0.2 * u[:, None]),
            "decay": bf(np.random.permutation(np.linspace(0.8, 1.04, H))),
            "out_w": bf(np.random.standard_normal((E, E)) / np.sqrt(E) / np.repeat(u, HD)[:, None]),
            "out_b": bf(np.random.standard_normal(E) * 0.2),
            "x": bf(np.random.standard_normal((B, T, E)))}


def reference(p, mix_w, mix_b, decay, out_w, out_b, x):
    m = mix_matrices(f64(mix_w), f64(decay))
    pq = mxq(f64(p), 2, "e4m3")
    cols = []
    for s0 in range(0, T, KB):
        s1 = s0 + KB
        mq = mxq(m[:, :s1, s0:s1], 1, "e4m3")
        cols.append(mq.transpose(0, 2, 1) @ pq[:, :, :s1, :])
    mixed = np.concatenate(cols, axis=2) + f64(mix_b)[None, :, :, None]
    c = mixed.transpose(0, 2, 1, 3).reshape(B, T, E)
    y = (mxq(c, 2, "e4m3") @ mxq(f64(out_w), 0, "e4m3")) + f64(out_b)
    return y + f64(x)

@@ -1,0 +1,284 @@
+from contextlib import ExitStack
+
+import concourse.mybir as mybir
+from concourse.masks import make_identity
+
+F32 = mybir.dt.float32
+BF16 = mybir.dt.bfloat16
+I32 = mybir.dt.int32
+U32 = mybir.dt.uint32
+U8 = mybir.dt.uint8
+FP8X4 = mybir.dt.float8_e4m3fn_x4
+ALU = mybir.AluOpType
+ACT = mybir.ActivationFunctionType
+
+P = 128
+PACK = 4
+K_PASS = P * PACK
+B, H, T, HD = 2, 16, 1024, 64
+E = H * HD
+HALF = H // 2
+CHUNKS = T // P
+PAIRS = H // 2
+N_TILE = 512
+PIECES = 3
+PIECE_OF = {(0, 0): 0, (0, 1): 1, (1, 1): 2}
+
+FLOPS = 2 * B * H * HD * (K_PASS * N_TILE + T * N_TILE) + 2 * B * T * E * E
+
+
+def regroup(engine_copy, grouped, planes):
+    engine_copy(
+        out=grouped.rearrange("q (c i) j -> q c j i", i=4),
+        in_=planes.rearrange("q j (c i) -> q c j i", i=4),
+    )
+
+
+def tile_mixerblock_pa_kernel(tc, p, mix_w, mix_b, decay, out_w, out_b, x, out):
+    nc = tc.nc
+    with ExitStack() as stack:
+        def pool(name, bufs):
+            return stack.enter_context(tc.tile_pool(name=name, bufs=bufs))
+
+        const = pool("const", 1)
+        right_pool = pool("right", 2)
+        wrow_pool = pool("wrow", 2)
+        grouped_pool = pool("grouped", 3)
+        m_pool = pool("m_words", 3)
+        p_pool = pool("p_stage", 2)
+        bias_pool = pool("bias_rows", 2)
+        c_pool = pool("c_planes", 6)
+        w_pool = pool("w_stage", 1)
+        x_pool = pool("x_stage", 2)
+        y_pool = pool("y_stage", 3)
+        psum_setup = stack.enter_context(tc.psum_pool(name="psum_setup", bufs=1))
+        psum_mix = stack.enter_context(tc.psum_pool(name="psum_mix", bufs=4))
+        psum_out = stack.enter_context(tc.psum_pool(name="psum_out", bufs=3))
+
+        s_int = const.tile([P, T], I32)
+        nc.gpsimd.iota(s_int[:], pattern=[[1, T]], base=0, channel_multiplier=0)
+        s_index = const.tile([P, T], F32)
+        nc.vector.tensor_copy(out=s_index[:], in_=s_int[:])
+        t_int = const.tile([P, CHUNKS], I32)
+        nc.gpsimd.iota(t_int[:], pattern=[[P, CHUNKS]], base=0, channel_multiplier=1)
+        t_index = const.tile([P, CHUNKS], F32)
+        nc.vector.tensor_copy(out=t_index[:], in_=t_int[:])
+        triangle = const.tile([P, P], BF16)
+        nc.vector.tensor_scalar(
+            out=triangle[:], in0=s_index[:, 0:P], scalar1=t_index[:, 0:1], scalar2=None, op0=ALU.is_ge
+        )
+        identity = const.tile([P, P], BF16)
+        make_identity(nc, identity[:])
+
+        decay_rows = const.tile([P, H], BF16)
+        nc.sync.dma_start(out=decay_rows[:], in_=decay.partition_broadcast(P))
+        d_clipped = const.tile([P, H], F32)
+        nc.vector.tensor_scalar(
+            out=d_clipped[:], in0=decay_rows[:], scalar1=0.9, scalar2=1.0, op0=ALU.max, op1=ALU.min
+        )
+        log_d = const.tile([P, H], F32)
+        nc.scalar.activation(out=log_d[:], in_=d_clipped[:], func=ACT.Ln)
+        half_log_d = const.tile([P, H], F32)
+        nc.vector.tensor_scalar_mul(out=half_log_d[:], in0=log_d[:], scalar1=0.5)
+        minus_half_log_d = const.tile([P, H], F32)
+        nc.vector.tensor_scalar_mul(out=minus_half_log_d[:], in0=log_d[:], scalar1=-0.5)
+
+        w_rows = const.tile([P, P], BF16)
+        nc.sync.dma_start(out=w_rows[:], in_=mix_w.rearrange("h (a q) -> (h a) q", q=P))
+        w_turned = psum_setup.tile([P, P], BF16)
+        nc.tensor.transpose(out=w_turned[:], in_=w_rows[:], identity=identity[:])
+        w_by_t = const.tile([P, H, CHUNKS], F32)
+        nc.vector.tensor_copy(out=w_by_t[:].rearrange("q h a -> q (h a)"), in_=w_turned[:])
+
+        left = const.tile([P, H, CHUNKS], F32)
+        nc.vector.tensor_tensor(
+            out=left[:],
+            in0=t_index[:].unsqueeze(1).to_broadcast([P, H, CHUNKS]),
+            in1=minus_half_log_d[:].unsqueeze(2).to_broadcast([P, H, CHUNKS]),
+            op=ALU.mult,
+        )
+        nc.scalar.activation(out=left[:], in_=left[:], func=ACT.Exp)
+        nc.vector.tensor_tensor(
+            out=left[:, HALF:H, :], in0=left[:, HALF:H, :], in1=w_by_t[:, HALF:H, :], op=ALU.mult
+        )
+
+        out_b_rows = const.tile([P, E], BF16)
+        nc.sync.dma_start(out=out_b_rows[:], in_=out_b.partition_broadcast(P))
+
+        m_low, m_high, diag_low, diag_high = [], [], [], []
+        for turn in range(2):
+            low_flat = const.tile([P, PACK * (T + P)], BF16, name="low_flat%d" % turn)
+            high_flat = const.tile([P, PACK * (K_PASS + P)], BF16, name="high_flat%d" % turn)
+            m_low.append(low_flat[:, 0 : PACK * T].rearrange("q (j s) -> q j s", j=PACK))
+            m_high.append(high_flat[:, 0 : PACK * K_PASS].rearrange("q (j s) -> q j s", j=PACK))
+            diag_low.append(low_flat[:].rearrange("q (j s) -> q j s", j=PACK)[:, :, 0:P])
+            diag_high.append(high_flat[:].rearrange("q (j s) -> q j s", j=PACK)[:, :, 0:P])
+            for j in range(1, PACK):
+                nc.vector.memset(m_low[turn][:, j, 0 : P * j], 0.0)
+                nc.vector.memset(m_high[turn][:, j, 0 : P * j], 0.0)
+
+        p_words, p_scales = [], []
+        for turn in range(2):
+            words = const.tile([P, B * 2, 3 * HD], U32, name="p_words%d" % turn, align_bytes=64)
+            scales = const.tile([P, B * 2, 3 * HD], U8, name="p_scales%d" % turn, align_bytes=64)
+            nc.vector.memset(words[:].bitcast(I32), 0)
+            nc.vector.memset(scales[:].bitcast(I32), 0)
+            p_words.append(words)
+            p_scales.append(scales)
+
+        c_words = const.tile([P, B, 2, T], U32, align_bytes=64)
+        c_scales = const.tile([P, B, 2, T], U8, align_bytes=64)
+        w_words = const.tile([P, 2, E], U32, align_bytes=64)
+        w_scales = const.tile([P, 2, E], U8, align_bytes=64)
+
+        for g in range(2):
+            w_raw = w_pool.tile([P, PACK, E], BF16)
+            nc.sync.dma_start(
+                out=w_raw[:],
+                in_=out_w[g * K_PASS : (g + 1) * K_PASS, :].rearrange("(j q) n -> q j n", q=P),
+            )
+            w_grouped = w_pool.tile([P, E, PACK], BF16, align_bytes=64)
+            regroup(nc.scalar.copy, w_grouped[:], w_raw[:])
+            nc.vector.quantize_mx(
+                out=w_words[:, g, :].bitcast(FP8X4),
+                scales=w_scales[:, g, :],
+                in_=w_grouped[:].rearrange("q n j -> q (n j)"),
+            )
+
+        c_planes = {}
+        for pair in range(PAIRS):
+            turn = pair % 2
+            p_raw = p_pool.tile([P, B, 2 * CHUNKS, HD], BF16)
+            for b in range(B):
+                nc.sync.dma_start(
+                    out=p_raw[:, b, :, :],
+                    in_=p[b, 2 * pair : 2 * pair + 2, :, :].rearrange("h (a q) f -> q (h a) f", q=P),
+                )
+            p_grouped = p_pool.tile([P, B, 2 * 2, HD, PACK], BF16, align_bytes=64)
+            for b in range(B):
+                nc.scalar.copy(
+                    out=p_grouped[:, b, :, :, :],
+                    in_=p_raw[:, b, :, :].rearrange("q (g j) f -> q g f j", j=PACK),
+                )
+            for b in range(B):
+                for odd in range(2):
+                    for c in range(2):
+                        cols = slice(2 * HD * odd, 2 * HD * odd + HD)
+                        nc.vector.quantize_mx(
+                            out=p_words[turn][:, 2 * b + c, cols].bitcast(FP8X4),
+                            scales=p_scales[turn][:, 2 * b + c, cols],
+                            in_=p_grouped[:, b, 2 * odd + c, :, :].rearrange("q f j -> q (f j)"),
+                        )
+
+            bias_rows = bias_pool.tile([P, T], BF16)
+            for odd in range(2):
+                nc.sync.dma_start(
+                    out=bias_rows[HD * odd : HD * (odd + 1), :],
+                    in_=mix_b[2 * pair + odd, :].partition_broadcast(HD),
+                )
+
+            m_words, m_scales = [], []
+            for odd in range(2):
+                h = 2 * pair + odd
+                low, high = m_low[odd], m_high[odd]
+                right = right_pool.tile([P, T], F32)
+                nc.scalar.activation(
+                    out=right[:], in_=s_index[:], func=ACT.Exp, scale=half_log_d[:, h : h + 1]
+                )
+                if h < HALF:
+                    w_row = wrow_pool.tile([P, T], BF16)
+                    nc.sync.dma_start(out=w_row[:], in_=mix_w[h, :].partition_broadcast(P))
+                    nc.vector.tensor_tensor(out=right[:], in0=right[:], in1=w_row[:], op=ALU.mult)
+                for a in range(CHUNKS):
+                    first = P * a
+                    if a < PACK:
+                        target = low[:, a, first:T]
+                    else:
+                        target = high[:, a - PACK, first - K_PASS : K_PASS]
+                    nc.scalar.activation(
+                        out=target, in_=right[:, first:T], func=ACT.Copy, scale=left[:, h, a : a + 1]
+                    )
+                for diag in (diag_low[odd], diag_high[odd]):
+                    nc.vector.tensor_tensor(
+                        out=diag,
+                        in0=diag,
+                        in1=triangle[:].unsqueeze(1).to_broadcast([P, PACK, P]),
+                        op=ALU.mult,
+                    )
+                words = m_pool.tile([P, PIECES, N_TILE], U32, align_bytes=64)
+                scales = m_pool.tile([P, PIECES, N_TILE], U8, align_bytes=64)
+                sources = (low[:, :, 0:N_TILE], low[:, :, N_TILE:T], high)
+                for piece in range(PIECES):
+                    m_grouped = grouped_pool.tile([P, N_TILE, PACK], BF16, tag="grouped", align_bytes=64)
+                    regroup(nc.vector.tensor_copy, m_grouped[:], sources[piece])
+                    nc.vector.quantize_mx(
+                        out=words[:, piece, :].bitcast(FP8X4),
+                        scales=scales[:, piece, :],
+                        in_=m_grouped[:].rearrange("q s j -> q (s j)"),
+                    )
+                m_words.append(words)
+                m_scales.append(scales)
+
+            for b in range(B):
+                for half in range(2):
+                    passes = [(odd, c) for odd in range(2) for c in range(half + 1)]
+                    mixed = psum_mix.tile([P, N_TILE], F32)
+                    for i, (odd, c) in enumerate(passes):
+                        cols = slice(HD * odd, HD * odd + P)
+                        piece = PIECE_OF[(c, half)]
+                        nc.tensor.matmul_mx(
+                            out=mixed[:],
+                            lhsT=p_words[turn][:, 2 * b + c, cols].bitcast(FP8X4),
+                            lhsT_scale=p_scales[turn][:, 2 * b + c, cols],
+                            rhs=m_words[odd][:, piece, :].bitcast(FP8X4),
+                            rhs_scale=m_scales[odd][:, piece, :],
+                            start=(i == 0),
+                            stop=(i == len(passes) - 1),
+                        )
+                    if pair % PACK == 0:
+                        c_planes[(b, half)] = c_pool.tile([P, PACK, N_TILE], BF16, name="c_planes")
+                    nc.vector.tensor_tensor(
+                        out=c_planes[(b, half)][:, pair % PACK, :],
+                        in0=mixed[:],
+                        in1=bias_rows[:, half * N_TILE : (half + 1) * N_TILE],
+                        op=ALU.add,
+                    )
+
+            if pair % PACK == PACK - 1:
+                g = pair // PACK
+                for b in range(B):
+                    for half in range(2):
+                        c_grouped = grouped_pool.tile([P, N_TILE, PACK], BF16, tag="grouped", align_bytes=64)
+                        regroup(nc.vector.tensor_copy, c_grouped[:], c_planes[(b, half)][:])
+                        cols = slice(half * N_TILE, (half + 1) * N_TILE)
+                        nc.vector.quantize_mx(
+                            out=c_words[:, b, g, cols].bitcast(FP8X4),
+                            scales=c_scales[:, b, g, cols],
+                            in_=c_grouped[:].rearrange("q s j -> q (s j)"),
+                        )
+
+        for b in range(B):
+            for block in range(T // P):
+                rows = slice(block * P, (block + 1) * P)
+                x_raw = x_pool.tile([P, E], BF16)
+                nc.sync.dma_start(out=x_raw[:], in_=x[b, rows, :])
+                x_plus_b = x_pool.tile([P, E], F32)
+                nc.vector.tensor_tensor(out=x_plus_b[:], in0=x_raw[:], in1=out_b_rows[:], op=ALU.add)
+                y = y_pool.tile([P, E], F32)
+                for half in range(2):
+                    cols = slice(half * N_TILE, (half + 1) * N_TILE)
+                    projected = psum_out.tile([P, N_TILE], F32)
+                    for g in range(2):
+                        nc.tensor.matmul_mx(
+                            out=projected[:],
+                            lhsT=c_words[:, b, g, rows].bitcast(FP8X4),
+                            lhsT_scale=c_scales[:, b, g, rows],
+                            rhs=w_words[:, g, cols].bitcast(FP8X4),
+                            rhs_scale=w_scales[:, g, cols],
+                            start=(g == 0),
+                            stop=(g == 1),
+                        )
+                    nc.vector.tensor_tensor(
+                        out=y[:, cols], in0=projected[:], in1=x_plus_b[:, cols], op=ALU.add
+                    )
+                nc.sync.dma_start(out=out[b, rows, :], in_=y[:])

@@ -17,12 +17,12 @@ PACK = 4
 K_PASS = P * PACK
 B, H, T, HD = 2, 16, 1024, 64
 E = H * HD
-HALF = H // 2
+HALF_H = H // 2
 CHUNKS = T // P
 PAIRS = H // 2
 N_TILE = 512
-PIECES = 3
-PIECE_OF = {(0, 0): 0, (0, 1): 1, (1, 1): 2}
+SWEEPS = T // N_TILE
+BLOCKS = N_TILE // P
 
 FLOPS = 2 * B * H * HD * (K_PASS * N_TILE + T * N_TILE) + 2 * B * T * E * E
 
@@ -41,34 +41,35 @@ def tile_mixerblock_pa_kernel(tc, p, mix_w, mix_b, decay, out_w, out_b, x, out):
             return stack.enter_context(tc.tile_pool(name=name, bufs=bufs))
 
         const = pool("const", 1)
-        right_pool = pool("right", 2)
-        wrow_pool = pool("wrow", 2)
         grouped_pool = pool("grouped", 3)
-        m_pool = pool("m_words", 3)
+        m_pool = pool("m_words", 6)
         p_pool = pool("p_stage", 2)
         bias_pool = pool("bias_rows", 2)
-        c_pool = pool("c_planes", 6)
+        c_pool = pool("c_planes", 4)
         w_pool = pool("w_stage", 1)
         x_pool = pool("x_stage", 2)
+        xb_pool = pool("x_plus_b", B * BLOCKS)
         y_pool = pool("y_stage", 3)
-        psum_setup = stack.enter_context(tc.psum_pool(name="psum_setup", bufs=1))
-        psum_mix = stack.enter_context(tc.psum_pool(name="psum_mix", bufs=4))
+        psum_right = stack.enter_context(tc.psum_pool(name="psum_right", bufs=2))
+        psum_mix = stack.enter_context(tc.psum_pool(name="psum_mix", bufs=3))
         psum_out = stack.enter_context(tc.psum_pool(name="psum_out", bufs=3))
 
-        s_int = const.tile([P, T], I32)
-        nc.gpsimd.iota(s_int[:], pattern=[[1, T]], base=0, channel_multiplier=0)
-        s_index = const.tile([P, T], F32)
-        nc.vector.tensor_copy(out=s_index[:], in_=s_int[:])
+        column_int = const.tile([P, P], I32)
+        nc.gpsimd.iota(column_int[:], pattern=[[1, P]], base=0, channel_multiplier=0)
+        column = const.tile([P, P], F32)
+        nc.vector.tensor_copy(out=column[:], in_=column_int[:])
         t_int = const.tile([P, CHUNKS], I32)
         nc.gpsimd.iota(t_int[:], pattern=[[P, CHUNKS]], base=0, channel_multiplier=1)
         t_index = const.tile([P, CHUNKS], F32)
         nc.vector.tensor_copy(out=t_index[:], in_=t_int[:])
         triangle = const.tile([P, P], BF16)
         nc.vector.tensor_scalar(
-            out=triangle[:], in0=s_index[:, 0:P], scalar1=t_index[:, 0:1], scalar2=None, op0=ALU.is_ge
+            out=triangle[:], in0=column[:], scalar1=t_index[:, 0:1], scalar2=None, op0=ALU.is_ge
         )
-        identity = const.tile([P, P], BF16)
-        make_identity(nc, identity[:])
+        identity_bf16 = const.tile([P, P], BF16)
+        make_identity(nc, identity_bf16[:])
+        identity_f32 = const.tile([P, P], F32)
+        make_identity(nc, identity_f32[:])
 
         decay_rows = const.tile([P, H], BF16)
         nc.sync.dma_start(out=decay_rows[:], in_=decay.partition_broadcast(P))
@@ -78,60 +79,78 @@ def tile_mixerblock_pa_kernel(tc, p, mix_w, mix_b, decay, out_w, out_b, x, out):
         )
         log_d = const.tile([P, H], F32)
         nc.scalar.activation(out=log_d[:], in_=d_clipped[:], func=ACT.Ln)
-        half_log_d = const.tile([P, H], F32)
-        nc.vector.tensor_scalar_mul(out=half_log_d[:], in0=log_d[:], scalar1=0.5)
-        minus_half_log_d = const.tile([P, H], F32)
-        nc.vector.tensor_scalar_mul(out=minus_half_log_d[:], in0=log_d[:], scalar1=-0.5)
 
         w_rows = const.tile([P, P], BF16)
         nc.sync.dma_start(out=w_rows[:], in_=mix_w.rearrange("h (a q) -> (h a) q", q=P))
-        w_turned = psum_setup.tile([P, P], BF16)
-        nc.tensor.transpose(out=w_turned[:], in_=w_rows[:], identity=identity[:])
+        w_turned = psum_right.tile([P, P], BF16, tag="right")
+        nc.tensor.transpose(out=w_turned[:], in_=w_rows[:], identity=identity_bf16[:])
         w_by_t = const.tile([P, H, CHUNKS], F32)
         nc.vector.tensor_copy(out=w_by_t[:].rearrange("q h a -> q (h a)"), in_=w_turned[:])
 
-        left = const.tile([P, H, CHUNKS], F32)
+        exponent = const.tile([P, H, CHUNKS], F32)
         nc.vector.tensor_tensor(
-            out=left[:],
+            out=exponent[:],
             in0=t_index[:].unsqueeze(1).to_broadcast([P, H, CHUNKS]),
-            in1=minus_half_log_d[:].unsqueeze(2).to_broadcast([P, H, CHUNKS]),
+            in1=log_d[:].unsqueeze(2).to_broadcast([P, H, CHUNKS]),
             op=ALU.mult,
         )
-        nc.scalar.activation(out=left[:], in_=left[:], func=ACT.Exp)
+        right = const.tile([P, H, CHUNKS], F32)
+        nc.scalar.activation(out=right[:], in_=exponent[:], func=ACT.Exp, scale=0.5)
+        left = const.tile([P, H, CHUNKS], F32)
+        nc.scalar.activation(out=left[:], in_=exponent[:], func=ACT.Exp, scale=-0.5)
         nc.vector.tensor_tensor(
-            out=left[:, HALF:H, :], in0=left[:, HALF:H, :], in1=w_by_t[:, HALF:H, :], op=ALU.mult
+            out=right[:, 0:HALF_H, :], in0=right[:, 0:HALF_H, :], in1=w_by_t[:, 0:HALF_H, :], op=ALU.mult
+        )
+        nc.vector.tensor_tensor(
+            out=left[:, HALF_H:H, :], in0=left[:, HALF_H:H, :], in1=w_by_t[:, HALF_H:H, :], op=ALU.mult
         )
 
         out_b_rows = const.tile([P, E], BF16)
         nc.sync.dma_start(out=out_b_rows[:], in_=out_b.partition_broadcast(P))
 
-        m_low, m_high, diag_low, diag_high = [], [], [], []
-        for turn in range(2):
-            low_flat = const.tile([P, PACK * (T + P)], BF16, name="low_flat%d" % turn)
-            high_flat = const.tile([P, PACK * (K_PASS + P)], BF16, name="high_flat%d" % turn)
-            m_low.append(low_flat[:, 0 : PACK * T].rearrange("q (j s) -> q j s", j=PACK))
-            m_high.append(high_flat[:, 0 : PACK * K_PASS].rearrange("q (j s) -> q j s", j=PACK))
-            diag_low.append(low_flat[:].rearrange("q (j s) -> q j s", j=PACK)[:, :, 0:P])
-            diag_high.append(high_flat[:].rearrange("q (j s) -> q j s", j=PACK)[:, :, 0:P])
+        full_piece, diag_piece, diag_blocks = [], [], []
+        for odd in range(2):
+            full = const.tile([P, PACK, N_TILE], BF16, name="full_piece%d" % odd)
+            flat = const.tile([P, PACK * (N_TILE + P)], BF16, name="diag_piece%d" % odd)
+            full_piece.append(full[:])
+            diag_piece.append(flat[:, 0 : PACK * N_TILE].rearrange("q (j s) -> q j s", j=PACK))
+            diag_blocks.append(flat[:].rearrange("q (j s) -> q j s", j=PACK)[:, :, 0:P])
             for j in range(1, PACK):
-                nc.vector.memset(m_low[turn][:, j, 0 : P * j], 0.0)
-                nc.vector.memset(m_high[turn][:, j, 0 : P * j], 0.0)
+                nc.vector.memset(diag_piece[odd][:, j, 0 : P * j], 0.0)
 
-        p_words, p_scales = [], []
-        for turn in range(2):
-            words = const.tile([P, B * 2, 3 * HD], U32, name="p_words%d" % turn, align_bytes=64)
-            scales = const.tile([P, B * 2, 3 * HD], U8, name="p_scales%d" % turn, align_bytes=64)
-            nc.vector.memset(words[:].bitcast(I32), 0)
-            nc.vector.memset(scales[:].bitcast(I32), 0)
-            p_words.append(words)
-            p_scales.append(scales)
+        p_words = const.tile([P, PAIRS, B * 2, 3 * HD], U32, align_bytes=64)
+        p_scales = const.tile([P, PAIRS, B * 2, 3 * HD], U8, align_bytes=64)
+        nc.vector.memset(p_words[:, :, :, HD : 2 * HD].bitcast(I32), 0)
+        nc.vector.memset(p_scales[:, :, :, HD : 2 * HD].bitcast(I32), 0)
 
         c_words = const.tile([P, B, 2, T], U32, align_bytes=64)
         c_scales = const.tile([P, B, 2, T], U8, align_bytes=64)
         w_words = const.tile([P, 2, E], U32, align_bytes=64)
         w_scales = const.tile([P, 2, E], U8, align_bytes=64)
 
-        for g in range(2):
+        def quantise_p(pair):
+            p_raw = p_pool.tile([P, B, 2 * CHUNKS, HD], BF16)
+            p_grouped = p_pool.tile([P, B, 2 * 2, HD, PACK], BF16, align_bytes=64)
+            for b in range(B):
+                nc.sync.dma_start(
+                    out=p_raw[:, b, :, :],
+                    in_=p[b, 2 * pair : 2 * pair + 2, :, :].rearrange("h (a q) f -> q (h a) f", q=P),
+                )
+                nc.scalar.copy(
+                    out=p_grouped[:, b, :, :, :],
+                    in_=p_raw[:, b, :, :].rearrange("q (g j) f -> q g f j", j=PACK),
+                )
+            for b in range(B):
+                for odd in range(2):
+                    for c in range(2):
+                        cols = slice(2 * HD * odd, 2 * HD * odd + HD)
+                        nc.vector.quantize_mx(
+                            out=p_words[:, pair, 2 * b + c, cols].bitcast(FP8X4),
+                            scales=p_scales[:, pair, 2 * b + c, cols],
+                            in_=p_grouped[:, b, 2 * odd + c, :, :].rearrange("q f j -> q (f j)"),
+                        )
+
+        def quantise_out_w(g):
             w_raw = w_pool.tile([P, PACK, E], BF16)
             nc.sync.dma_start(
                 out=w_raw[:],
@@ -145,140 +164,125 @@ def tile_mixerblock_pa_kernel(tc, p, mix_w, mix_b, decay, out_w, out_b, x, out):
                 in_=w_grouped[:].rearrange("q n j -> q (n j)"),
             )
 
-        c_planes = {}
-        for pair in range(PAIRS):
-            turn = pair % 2
-            p_raw = p_pool.tile([P, B, 2 * CHUNKS, HD], BF16)
-            for b in range(B):
-                nc.sync.dma_start(
-                    out=p_raw[:, b, :, :],
-                    in_=p[b, 2 * pair : 2 * pair + 2, :, :].rearrange("h (a q) f -> q (h a) f", q=P),
+        def make_piece(h, c, right_rows, on_diagonal):
+            odd = h % 2
+            planes = diag_piece[odd] if on_diagonal else full_piece[odd]
+            for j in range(PACK):
+                first = P * j if on_diagonal else 0
+                nc.scalar.activation(
+                    out=planes[:, j, first:N_TILE],
+                    in_=right_rows[:, first:N_TILE],
+                    func=ACT.Copy,
+                    scale=left[:, h, PACK * c + j : PACK * c + j + 1],
                 )
-            p_grouped = p_pool.tile([P, B, 2 * 2, HD, PACK], BF16, align_bytes=64)
-            for b in range(B):
-                nc.scalar.copy(
-                    out=p_grouped[:, b, :, :, :],
-                    in_=p_raw[:, b, :, :].rearrange("q (g j) f -> q g f j", j=PACK),
+            if on_diagonal:
+                nc.vector.tensor_tensor(
+                    out=diag_blocks[odd],
+                    in0=diag_blocks[odd],
+                    in1=triangle[:].unsqueeze(1).to_broadcast([P, PACK, P]),
+                    op=ALU.mult,
                 )
-            for b in range(B):
-                for odd in range(2):
-                    for c in range(2):
-                        cols = slice(2 * HD * odd, 2 * HD * odd + HD)
-                        nc.vector.quantize_mx(
-                            out=p_words[turn][:, 2 * b + c, cols].bitcast(FP8X4),
-                            scales=p_scales[turn][:, 2 * b + c, cols],
-                            in_=p_grouped[:, b, 2 * odd + c, :, :].rearrange("q f j -> q (f j)"),
-                        )
+            m_grouped = grouped_pool.tile([P, N_TILE, PACK], BF16, tag="grouped", align_bytes=64)
+            regroup(nc.vector.tensor_copy, m_grouped[:], planes)
+            words = m_pool.tile([P, N_TILE], U32, align_bytes=64)
+            scales = m_pool.tile([P, N_TILE], U8, align_bytes=64)
+            nc.vector.quantize_mx(
+                out=words[:].bitcast(FP8X4),
+                scales=scales[:],
+                in_=m_grouped[:].rearrange("q s j -> q (s j)"),
+            )
+            return words, scales
 
-            bias_rows = bias_pool.tile([P, T], BF16)
+        def mix(sweep, pair, c_planes):
+            steps = slice(sweep * N_TILE, (sweep + 1) * N_TILE)
+            bias_rows = bias_pool.tile([P, N_TILE], BF16)
             for odd in range(2):
                 nc.sync.dma_start(
                     out=bias_rows[HD * odd : HD * (odd + 1), :],
-                    in_=mix_b[2 * pair + odd, :].partition_broadcast(HD),
+                    in_=mix_b[2 * pair + odd, steps].partition_broadcast(HD),
                 )
-
-            m_words, m_scales = [], []
+            pieces = {}
             for odd in range(2):
                 h = 2 * pair + odd
-                low, high = m_low[odd], m_high[odd]
-                right = right_pool.tile([P, T], F32)
-                nc.scalar.activation(
-                    out=right[:], in_=s_index[:], func=ACT.Exp, scale=half_log_d[:, h : h + 1]
-                )
-                if h < HALF:
-                    w_row = wrow_pool.tile([P, T], BF16)
-                    nc.sync.dma_start(out=w_row[:], in_=mix_w[h, :].partition_broadcast(P))
-                    nc.vector.tensor_tensor(out=right[:], in0=right[:], in1=w_row[:], op=ALU.mult)
-                for a in range(CHUNKS):
-                    first = P * a
-                    if a < PACK:
-                        target = low[:, a, first:T]
-                    else:
-                        target = high[:, a - PACK, first - K_PASS : K_PASS]
-                    nc.scalar.activation(
-                        out=target, in_=right[:, first:T], func=ACT.Copy, scale=left[:, h, a : a + 1]
+                right_rows = psum_right.tile([P, N_TILE], F32, tag="right")
+                for i in range(BLOCKS):
+                    a = sweep * BLOCKS + i
+                    nc.tensor.transpose(
+                        out=right_rows[:, i * P : (i + 1) * P],
+                        in_=right[:, h, a : a + 1].to_broadcast([P, P]),
+                        identity=identity_f32[:],
                     )
-                for diag in (diag_low[odd], diag_high[odd]):
-                    nc.vector.tensor_tensor(
-                        out=diag,
-                        in0=diag,
-                        in1=triangle[:].unsqueeze(1).to_broadcast([P, PACK, P]),
-                        op=ALU.mult,
-                    )
-                words = m_pool.tile([P, PIECES, N_TILE], U32, align_bytes=64)
-                scales = m_pool.tile([P, PIECES, N_TILE], U8, align_bytes=64)
-                sources = (low[:, :, 0:N_TILE], low[:, :, N_TILE:T], high)
-                for piece in range(PIECES):
-                    m_grouped = grouped_pool.tile([P, N_TILE, PACK], BF16, tag="grouped", align_bytes=64)
-                    regroup(nc.vector.tensor_copy, m_grouped[:], sources[piece])
-                    nc.vector.quantize_mx(
-                        out=words[:, piece, :].bitcast(FP8X4),
-                        scales=scales[:, piece, :],
-                        in_=m_grouped[:].rearrange("q s j -> q (s j)"),
-                    )
-                m_words.append(words)
-                m_scales.append(scales)
-
+                for c in range(sweep + 1):
+                    pieces[(odd, c)] = make_piece(h, c, right_rows, on_diagonal=(c == sweep))
+            passes = [(odd, c) for odd in range(2) for c in range(sweep + 1)]
             for b in range(B):
-                for half in range(2):
-                    passes = [(odd, c) for odd in range(2) for c in range(half + 1)]
-                    mixed = psum_mix.tile([P, N_TILE], F32)
-                    for i, (odd, c) in enumerate(passes):
-                        cols = slice(HD * odd, HD * odd + P)
-                        piece = PIECE_OF[(c, half)]
-                        nc.tensor.matmul_mx(
-                            out=mixed[:],
-                            lhsT=p_words[turn][:, 2 * b + c, cols].bitcast(FP8X4),
-                            lhsT_scale=p_scales[turn][:, 2 * b + c, cols],
-                            rhs=m_words[odd][:, piece, :].bitcast(FP8X4),
-                            rhs_scale=m_scales[odd][:, piece, :],
-                            start=(i == 0),
-                            stop=(i == len(passes) - 1),
-                        )
-                    if pair % PACK == 0:
-                        c_planes[(b, half)] = c_pool.tile([P, PACK, N_TILE], BF16, name="c_planes")
-                    nc.vector.tensor_tensor(
-                        out=c_planes[(b, half)][:, pair % PACK, :],
-                        in0=mixed[:],
-                        in1=bias_rows[:, half * N_TILE : (half + 1) * N_TILE],
-                        op=ALU.add,
+                mixed = psum_mix.tile([P, N_TILE], F32)
+                for i, (odd, c) in enumerate(passes):
+                    cols = slice(HD * odd, HD * odd + P)
+                    words, scales = pieces[(odd, c)]
+                    nc.tensor.matmul_mx(
+                        out=mixed[:],
+                        lhsT=p_words[:, pair, 2 * b + c, cols].bitcast(FP8X4),
+                        lhsT_scale=p_scales[:, pair, 2 * b + c, cols],
+                        rhs=words[:].bitcast(FP8X4),
+                        rhs_scale=scales[:],
+                        start=(i == 0),
+                        stop=(i == len(passes) - 1),
                     )
+                nc.vector.tensor_tensor(
+                    out=c_planes[b][:, pair % PACK, :], in0=mixed[:], in1=bias_rows[:], op=ALU.add
+                )
 
-            if pair % PACK == PACK - 1:
-                g = pair // PACK
-                for b in range(B):
-                    for half in range(2):
-                        c_grouped = grouped_pool.tile([P, N_TILE, PACK], BF16, tag="grouped", align_bytes=64)
-                        regroup(nc.vector.tensor_copy, c_grouped[:], c_planes[(b, half)][:])
-                        cols = slice(half * N_TILE, (half + 1) * N_TILE)
-                        nc.vector.quantize_mx(
-                            out=c_words[:, b, g, cols].bitcast(FP8X4),
-                            scales=c_scales[:, b, g, cols],
-                            in_=c_grouped[:].rearrange("q s j -> q (s j)"),
-                        )
+        def quantise_c(sweep, g, c_planes):
+            cols = slice(sweep * N_TILE, (sweep + 1) * N_TILE)
+            for b in range(B):
+                c_grouped = grouped_pool.tile([P, N_TILE, PACK], BF16, tag="grouped", align_bytes=64)
+                regroup(nc.scalar.copy, c_grouped[:], c_planes[b][:])
+                nc.vector.quantize_mx(
+                    out=c_words[:, b, g, cols].bitcast(FP8X4),
+                    scales=c_scales[:, b, g, cols],
+                    in_=c_grouped[:].rearrange("q s j -> q (s j)"),
+                )
 
+        def project(b, block):
+            rows = slice(block * P, (block + 1) * P)
+            x_raw = x_pool.tile([P, E], BF16)
+            nc.sync.dma_start(out=x_raw[:], in_=x[b, rows, :])
+            x_plus_b = xb_pool.tile([P, E], F32)
+            nc.vector.tensor_tensor(out=x_plus_b[:], in0=x_raw[:], in1=out_b_rows[:], op=ALU.add)
+            y = y_pool.tile([P, E], F32)
+            for half in range(E // N_TILE):
+                cols = slice(half * N_TILE, (half + 1) * N_TILE)
+                projected = psum_out.tile([P, N_TILE], F32)
+                for g in range(2):
+                    nc.tensor.matmul_mx(
+                        out=projected[:],
+                        lhsT=c_words[:, b, g, rows].bitcast(FP8X4),
+                        lhsT_scale=c_scales[:, b, g, rows],
+                        rhs=w_words[:, g, cols].bitcast(FP8X4),
+                        rhs_scale=w_scales[:, g, cols],
+                        start=(g == 0),
+                        stop=(g == 1),
+                    )
+                nc.vector.tensor_tensor(out=y[:, cols], in0=projected[:], in1=x_plus_b[:, cols], op=ALU.add)
+            nc.sync.dma_start(out=out[b, rows, :], in_=y[:])
+
+        for sweep in range(SWEEPS):
+            c_planes = []
+            for pair in range(PAIRS):
+                if sweep == 0:
+                    quantise_p(pair)
+                    if pair < E // K_PASS:
+                        quantise_out_w(pair)
+                else:
+                    project(pair // BLOCKS, pair % BLOCKS)
+                if pair % PACK == 0:
+                    c_planes = [
+                        c_pool.tile([P, PACK, N_TILE], BF16, name="c_planes") for b in range(B)
+                    ]
+                mix(sweep, pair, c_planes)
+                if pair % PACK == PACK - 1:
+                    quantise_c(sweep, pair // PACK, c_planes)
         for b in range(B):
-            for block in range(T // P):
-                rows = slice(block * P, (block + 1) * P)
-                x_raw = x_pool.tile([P, E], BF16)
-                nc.sync.dma_start(out=x_raw[:], in_=x[b, rows, :])
-                x_plus_b = x_pool.tile([P, E], F32)
-                nc.vector.tensor_tensor(out=x_plus_b[:], in0=x_raw[:], in1=out_b_rows[:], op=ALU.add)
-                y = y_pool.tile([P, E], F32)
-                for half in range(2):
-                    cols = slice(half * N_TILE, (half + 1) * N_TILE)
-                    projected = psum_out.tile([P, N_TILE], F32)
-                    for g in range(2):
-                        nc.tensor.matmul_mx(
-                            out=projected[:],
-                            lhsT=c_words[:, b, g, rows].bitcast(FP8X4),
-                            lhsT_scale=c_scales[:, b, g, rows],
-                            rhs=w_words[:, g, cols].bitcast(FP8X4),
-                            rhs_scale=w_scales[:, g, cols],
-                            start=(g == 0),
-                            stop=(g == 1),
-                        )
-                    nc.vector.tensor_tensor(
-                        out=y[:, cols], in0=projected[:], in1=x_plus_b[:, cols], op=ALU.add
-                    )
-                nc.sync.dma_start(out=out[b, rows, :], in_=y[:])
+            for block in range(BLOCKS, 2 * BLOCKS):
+                project(b, block)

@@ -47,12 +47,13 @@ def tile_mixerblock_pa_kernel(tc, p, mix_w, mix_b, decay, out_w, out_b, x, out):
         bias_pool = pool("bias_rows", 2)
         c_pool = pool("c_planes", 4)
         w_pool = pool("w_stage", 1)
-        x_pool = pool("x_stage", 2)
-        xb_pool = pool("x_plus_b", B * BLOCKS)
+        x_pool = pool("x_stage", 3)
+        turned_pool = pool("y_turned", 2)
         y_pool = pool("y_stage", 3)
         psum_right = stack.enter_context(tc.psum_pool(name="psum_right", bufs=2))
-        psum_mix = stack.enter_context(tc.psum_pool(name="psum_mix", bufs=3))
-        psum_out = stack.enter_context(tc.psum_pool(name="psum_out", bufs=3))
+        psum_mix = stack.enter_context(tc.psum_pool(name="psum_mix", bufs=2))
+        psum_out = stack.enter_context(tc.psum_pool(name="psum_out", bufs=2))
+        psum_back = stack.enter_context(tc.psum_pool(name="psum_back", bufs=2))
 
         column_int = const.tile([P, P], I32)
         nc.gpsimd.iota(column_int[:], pattern=[[1, P]], base=0, channel_multiplier=0)
@@ -105,8 +106,13 @@ def tile_mixerblock_pa_kernel(tc, p, mix_w, mix_b, decay, out_w, out_b, x, out):
             out=left[:, HALF_H:H, :], in0=left[:, HALF_H:H, :], in1=w_by_t[:, HALF_H:H, :], op=ALU.mult
         )
 
-        out_b_rows = const.tile([P, E], BF16)
-        nc.sync.dma_start(out=out_b_rows[:], in_=out_b.partition_broadcast(P))
+        out_b_rows = const.tile([P, P], BF16)
+        nc.vector.memset(out_b_rows[:], 0.0)
+        nc.sync.dma_start(out=out_b_rows[0 : E // P, :], in_=out_b.rearrange("(i q) -> i q", q=P))
+        out_b_turned = psum_right.tile([P, P], BF16, tag="right")
+        nc.tensor.transpose(out=out_b_turned[:], in_=out_b_rows[:], identity=identity_bf16[:])
+        out_b_column = const.tile([P, E // P], F32)
+        nc.vector.tensor_copy(out=out_b_column[:], in_=out_b_turned[:, 0 : E // P])
 
         full_piece, diag_piece, diag_blocks = [], [], []
         for odd in range(2):
@@ -235,37 +241,54 @@ def tile_mixerblock_pa_kernel(tc, p, mix_w, mix_b, decay, out_w, out_b, x, out):
 
         def quantise_c(sweep, g, c_planes):
             cols = slice(sweep * N_TILE, (sweep + 1) * N_TILE)
+            copies = (nc.vector.tensor_copy, nc.scalar.copy)
             for b in range(B):
                 c_grouped = grouped_pool.tile([P, N_TILE, PACK], BF16, tag="grouped", align_bytes=64)
-                regroup(nc.scalar.copy, c_grouped[:], c_planes[b][:])
+                regroup(copies[b], c_grouped[:], c_planes[b][:])
                 nc.vector.quantize_mx(
                     out=c_words[:, b, g, cols].bitcast(FP8X4),
                     scales=c_scales[:, b, g, cols],
                     in_=c_grouped[:].rearrange("q s j -> q (s j)"),
                 )
 
-        def project(b, block):
-            rows = slice(block * P, (block + 1) * P)
-            x_raw = x_pool.tile([P, E], BF16)
-            nc.sync.dma_start(out=x_raw[:], in_=x[b, rows, :])
-            x_plus_b = xb_pool.tile([P, E], F32)
-            nc.vector.tensor_tensor(out=x_plus_b[:], in0=x_raw[:], in1=out_b_rows[:], op=ALU.add)
-            y = y_pool.tile([P, E], F32)
-            for half in range(E // N_TILE):
-                cols = slice(half * N_TILE, (half + 1) * N_TILE)
+        def project(b, sweep, n_half):
+            steps = slice(sweep * N_TILE, (sweep + 1) * N_TILE)
+            y_turned = turned_pool.tile([P, BLOCKS, N_TILE], F32)
+            for i in range(BLOCKS):
+                n_block = n_half * BLOCKS + i
+                cols = slice(n_block * P, (n_block + 1) * P)
                 projected = psum_out.tile([P, N_TILE], F32)
                 for g in range(2):
                     nc.tensor.matmul_mx(
                         out=projected[:],
-                        lhsT=c_words[:, b, g, rows].bitcast(FP8X4),
-                        lhsT_scale=c_scales[:, b, g, rows],
-                        rhs=w_words[:, g, cols].bitcast(FP8X4),
-                        rhs_scale=w_scales[:, g, cols],
+                        lhsT=w_words[:, g, cols].bitcast(FP8X4),
+                        lhsT_scale=w_scales[:, g, cols],
+                        rhs=c_words[:, b, g, steps].bitcast(FP8X4),
+                        rhs_scale=c_scales[:, b, g, steps],
                         start=(g == 0),
                         stop=(g == 1),
                     )
-                nc.vector.tensor_tensor(out=y[:, cols], in0=projected[:], in1=x_plus_b[:, cols], op=ALU.add)
-            nc.sync.dma_start(out=out[b, rows, :], in_=y[:])
+                nc.scalar.activation(
+                    out=y_turned[:, i, :],
+                    in_=projected[:],
+                    func=ACT.Identity,
+                    bias=out_b_column[:, n_block : n_block + 1],
+                )
+            n_cols = slice(n_half * N_TILE, (n_half + 1) * N_TILE)
+            for block in range(BLOCKS):
+                rows = slice(sweep * N_TILE + block * P, sweep * N_TILE + (block + 1) * P)
+                x_raw = x_pool.tile([P, N_TILE], BF16)
+                nc.sync.dma_start(out=x_raw[:], in_=x[b, rows, n_cols])
+                turned_back = psum_back.tile([P, N_TILE], F32)
+                for i in range(BLOCKS):
+                    nc.tensor.transpose(
+                        out=turned_back[:, i * P : (i + 1) * P],
+                        in_=y_turned[:, i, block * P : (block + 1) * P],
+                        identity=identity_f32[:],
+                    )
+                y = y_pool.tile([P, N_TILE], F32)
+                nc.vector.tensor_tensor(out=y[:], in0=turned_back[:], in1=x_raw[:], op=ALU.add)
+                nc.sync.dma_start(out=out[b, rows, n_cols], in_=y[:])
 
         for sweep in range(SWEEPS):
             c_planes = []
@@ -274,8 +297,8 @@ def tile_mixerblock_pa_kernel(tc, p, mix_w, mix_b, decay, out_w, out_b, x, out):
                     quantise_p(pair)
                     if pair < E // K_PASS:
                         quantise_out_w(pair)
-                else:
-                    project(pair // BLOCKS, pair % BLOCKS)
+                elif pair % 2 == 0:
+                    project(pair // PACK, 0, (pair // 2) % 2)
                 if pair % PACK == 0:
                     c_planes = [
                         c_pool.tile([P, PACK, N_TILE], BF16, name="c_planes") for b in range(B)
@@ -284,5 +307,5 @@ def tile_mixerblock_pa_kernel(tc, p, mix_w, mix_b, decay, out_w, out_b, x, out):
                 if pair % PACK == PACK - 1:
                     quantise_c(sweep, pair // PACK, c_planes)
         for b in range(B):
-            for block in range(BLOCKS, 2 * BLOCKS):
-                project(b, block)
+            for n_half in range(E // N_TILE):
+                project(b, 1, n_half)

@@ -23,6 +23,10 @@ PAIRS = H // 2
 N_TILE = 512
 SWEEPS = T // N_TILE
 BLOCKS = N_TILE // P
+UNITS = SWEEPS * H
+ROUNDS = SWEEPS * PAIRS
+ITEMS = SWEEPS * B * (E // N_TILE) * BLOCKS
+FIRST_ITEM = H + 2
 
 FLOPS = 2 * B * H * HD * (K_PASS * N_TILE + T * N_TILE) + 2 * B * T * E * E
 
@@ -41,14 +45,14 @@ def tile_mixerblock_pa_kernel(tc, p, mix_w, mix_b, decay, out_w, out_b, x, out):
             return stack.enter_context(tc.tile_pool(name=name, bufs=bufs))
 
         const = pool("const", 1)
-        grouped_pool = pool("grouped", 3)
+        grouped_pool = pool("grouped", 4)
         m_pool = pool("m_words", 6)
         p_pool = pool("p_stage", 2)
-        bias_pool = pool("bias_rows", 2)
+        bias_pool = pool("bias_rows", 3)
         c_pool = pool("c_planes", 4)
-        w_pool = pool("w_stage", 1)
-        x_pool = pool("x_stage", 3)
-        turned_pool = pool("y_turned", 2)
+        w_pool = pool("w_stage", 2)
+        x_pool = pool("x_stage", 5)
+        turned_pool = pool("y_turned", 3)
         y_pool = pool("y_stage", 3)
         psum_right = stack.enter_context(tc.psum_pool(name="psum_right", bufs=2))
         psum_mix = stack.enter_context(tc.psum_pool(name="psum_mix", bufs=2))
@@ -134,18 +138,35 @@ def tile_mixerblock_pa_kernel(tc, p, mix_w, mix_b, decay, out_w, out_b, x, out):
         w_words = const.tile([P, 2, E], U32, align_bytes=64)
         w_scales = const.tile([P, 2, E], U8, align_bytes=64)
 
-        def quantise_p(pair):
-            p_raw = p_pool.tile([P, B, 2 * CHUNKS, HD], BF16)
-            p_grouped = p_pool.tile([P, B, 2 * 2, HD, PACK], BF16, align_bytes=64)
+        p_raw, p_grouped, w_raw, bias_rows, right_rows = {}, {}, {}, {}, {}
+        m_grouped, m_words, m_scales, mixed, c_planes, c_grouped = {}, {}, {}, {}, {}, {}
+        projected, y_turned, turned_back, x_raw = {}, {}, {}, {}
+
+        def load_p(pair):
+            if not 0 <= pair < PAIRS:
+                return
+            p_raw[pair] = p_pool.tile([P, B, 2 * CHUNKS, HD], BF16, name="p_raw")
             for b in range(B):
                 nc.sync.dma_start(
-                    out=p_raw[:, b, :, :],
+                    out=p_raw[pair][:, b, :, :],
                     in_=p[b, 2 * pair : 2 * pair + 2, :, :].rearrange("h (a q) f -> q (h a) f", q=P),
                 )
+
+        def regroup_p(pair):
+            if not 0 <= pair < PAIRS:
+                return
+            p_grouped[pair] = p_pool.tile(
+                [P, B, 2 * 2, HD, PACK], BF16, name="p_grouped", align_bytes=64
+            )
+            for b in range(B):
                 nc.scalar.copy(
-                    out=p_grouped[:, b, :, :, :],
-                    in_=p_raw[:, b, :, :].rearrange("q (g j) f -> q g f j", j=PACK),
+                    out=p_grouped[pair][:, b, :, :, :],
+                    in_=p_raw[pair][:, b, :, :].rearrange("q (g j) f -> q g f j", j=PACK),
                 )
+
+        def quantise_p(pair):
+            if not 0 <= pair < PAIRS:
+                return
             for b in range(B):
                 for odd in range(2):
                     for c in range(2):
@@ -153,159 +174,246 @@ def tile_mixerblock_pa_kernel(tc, p, mix_w, mix_b, decay, out_w, out_b, x, out):
                         nc.vector.quantize_mx(
                             out=p_words[:, pair, 2 * b + c, cols].bitcast(FP8X4),
                             scales=p_scales[:, pair, 2 * b + c, cols],
-                            in_=p_grouped[:, b, 2 * odd + c, :, :].rearrange("q f j -> q (f j)"),
+                            in_=p_grouped[pair][:, b, 2 * odd + c, :, :].rearrange("q f j -> q (f j)"),
                         )
 
-        def quantise_out_w(g):
-            w_raw = w_pool.tile([P, PACK, E], BF16)
+        def load_out_w(g):
+            if not 0 <= g < E // K_PASS:
+                return
+            w_raw[g] = w_pool.tile([P, PACK, E], BF16, name="w_raw")
             nc.sync.dma_start(
-                out=w_raw[:],
+                out=w_raw[g][:],
                 in_=out_w[g * K_PASS : (g + 1) * K_PASS, :].rearrange("(j q) n -> q j n", q=P),
             )
+
+        def quantise_out_w(g):
+            if not 0 <= g < E // K_PASS:
+                return
             w_grouped = w_pool.tile([P, E, PACK], BF16, align_bytes=64)
-            regroup(nc.scalar.copy, w_grouped[:], w_raw[:])
+            regroup(nc.vector.tensor_copy, w_grouped[:], w_raw[g][:])
             nc.vector.quantize_mx(
                 out=w_words[:, g, :].bitcast(FP8X4),
                 scales=w_scales[:, g, :],
                 in_=w_grouped[:].rearrange("q n j -> q (n j)"),
             )
 
-        def make_piece(h, c, right_rows, on_diagonal):
-            odd = h % 2
-            planes = diag_piece[odd] if on_diagonal else full_piece[odd]
-            for j in range(PACK):
-                first = P * j if on_diagonal else 0
-                nc.scalar.activation(
-                    out=planes[:, j, first:N_TILE],
-                    in_=right_rows[:, first:N_TILE],
-                    func=ACT.Copy,
-                    scale=left[:, h, PACK * c + j : PACK * c + j + 1],
+        def spread_right(unit):
+            if not 0 <= unit < UNITS:
+                return
+            sweep, h = divmod(unit, H)
+            right_rows[unit] = psum_right.tile([P, N_TILE], F32, name="right_rows", tag="right")
+            for i in range(BLOCKS):
+                a = sweep * BLOCKS + i
+                nc.tensor.transpose(
+                    out=right_rows[unit][:, i * P : (i + 1) * P],
+                    in_=right[:, h, a : a + 1].to_broadcast([P, P]),
+                    identity=identity_f32[:],
                 )
-            if on_diagonal:
-                nc.vector.tensor_tensor(
-                    out=diag_blocks[odd],
-                    in0=diag_blocks[odd],
-                    in1=triangle[:].unsqueeze(1).to_broadcast([P, PACK, P]),
-                    op=ALU.mult,
-                )
-            m_grouped = grouped_pool.tile([P, N_TILE, PACK], BF16, tag="grouped", align_bytes=64)
-            regroup(nc.vector.tensor_copy, m_grouped[:], planes)
-            words = m_pool.tile([P, N_TILE], U32, align_bytes=64)
-            scales = m_pool.tile([P, N_TILE], U8, align_bytes=64)
-            nc.vector.quantize_mx(
-                out=words[:].bitcast(FP8X4),
-                scales=scales[:],
-                in_=m_grouped[:].rearrange("q s j -> q (s j)"),
-            )
-            return words, scales
 
-        def mix(sweep, pair, c_planes):
-            steps = slice(sweep * N_TILE, (sweep + 1) * N_TILE)
-            bias_rows = bias_pool.tile([P, N_TILE], BF16)
+        def planes_of(unit, c):
+            sweep, h = divmod(unit, H)
+            return diag_piece[h % 2] if c == sweep else full_piece[h % 2]
+
+        def write_chunks(unit):
+            if not 0 <= unit < UNITS:
+                return
+            sweep, h = divmod(unit, H)
+            for c in range(sweep + 1):
+                for j in range(PACK):
+                    first = P * j if c == sweep else 0
+                    nc.scalar.activation(
+                        out=planes_of(unit, c)[:, j, first:N_TILE],
+                        in_=right_rows[unit][:, first:N_TILE],
+                        func=ACT.Copy,
+                        scale=left[:, h, PACK * c + j : PACK * c + j + 1],
+                    )
+
+        def regroup_m(unit):
+            if not 0 <= unit < UNITS:
+                return
+            sweep, h = divmod(unit, H)
+            nc.vector.tensor_tensor(
+                out=diag_blocks[h % 2],
+                in0=diag_blocks[h % 2],
+                in1=triangle[:].unsqueeze(1).to_broadcast([P, PACK, P]),
+                op=ALU.mult,
+            )
+            for c in range(sweep + 1):
+                m_grouped[(unit, c)] = grouped_pool.tile(
+                    [P, N_TILE, PACK], BF16, name="m_grouped", tag="grouped", align_bytes=64
+                )
+                regroup(nc.vector.tensor_copy, m_grouped[(unit, c)][:], planes_of(unit, c))
+
+        def quantise_m(unit):
+            if not 0 <= unit < UNITS:
+                return
+            for c in range(unit // H + 1):
+                m_words[(unit, c)] = m_pool.tile([P, N_TILE], U32, name="m_words", align_bytes=64)
+                m_scales[(unit, c)] = m_pool.tile([P, N_TILE], U8, name="m_scales", align_bytes=64)
+                nc.vector.quantize_mx(
+                    out=m_words[(unit, c)][:].bitcast(FP8X4),
+                    scales=m_scales[(unit, c)][:],
+                    in_=m_grouped[(unit, c)][:].rearrange("q s j -> q (s j)"),
+                )
+
+        def load_bias(rnd):
+            if not 0 <= rnd < ROUNDS:
+                return
+            sweep, pair = divmod(rnd, PAIRS)
+            bias_rows[rnd] = bias_pool.tile([P, N_TILE], BF16, name="bias_rows")
             for odd in range(2):
                 nc.sync.dma_start(
-                    out=bias_rows[HD * odd : HD * (odd + 1), :],
-                    in_=mix_b[2 * pair + odd, steps].partition_broadcast(HD),
+                    out=bias_rows[rnd][HD * odd : HD * (odd + 1), :],
+                    in_=mix_b[2 * pair + odd, sweep * N_TILE : (sweep + 1) * N_TILE].partition_broadcast(HD),
                 )
-            pieces = {}
-            for odd in range(2):
-                h = 2 * pair + odd
-                right_rows = psum_right.tile([P, N_TILE], F32, tag="right")
-                for i in range(BLOCKS):
-                    a = sweep * BLOCKS + i
-                    nc.tensor.transpose(
-                        out=right_rows[:, i * P : (i + 1) * P],
-                        in_=right[:, h, a : a + 1].to_broadcast([P, P]),
-                        identity=identity_f32[:],
-                    )
-                for c in range(sweep + 1):
-                    pieces[(odd, c)] = make_piece(h, c, right_rows, on_diagonal=(c == sweep))
+
+        def multiply(rnd):
+            if not 0 <= rnd < ROUNDS:
+                return
+            sweep, pair = divmod(rnd, PAIRS)
             passes = [(odd, c) for odd in range(2) for c in range(sweep + 1)]
             for b in range(B):
-                mixed = psum_mix.tile([P, N_TILE], F32)
+                mixed[(rnd, b)] = psum_mix.tile([P, N_TILE], F32, name="mixed")
                 for i, (odd, c) in enumerate(passes):
                     cols = slice(HD * odd, HD * odd + P)
-                    words, scales = pieces[(odd, c)]
+                    unit = 2 * rnd + odd
                     nc.tensor.matmul_mx(
-                        out=mixed[:],
+                        out=mixed[(rnd, b)][:],
                         lhsT=p_words[:, pair, 2 * b + c, cols].bitcast(FP8X4),
                         lhsT_scale=p_scales[:, pair, 2 * b + c, cols],
-                        rhs=words[:].bitcast(FP8X4),
-                        rhs_scale=scales[:],
+                        rhs=m_words[(unit, c)][:].bitcast(FP8X4),
+                        rhs_scale=m_scales[(unit, c)][:],
                         start=(i == 0),
                         stop=(i == len(passes) - 1),
                     )
+
+        def add_bias(rnd):
+            if not 0 <= rnd < ROUNDS:
+                return
+            for b in range(B):
+                if rnd % PACK == 0:
+                    c_planes[(rnd // PACK, b)] = c_pool.tile([P, PACK, N_TILE], BF16, name="c_planes")
                 nc.vector.tensor_tensor(
-                    out=c_planes[b][:, pair % PACK, :], in0=mixed[:], in1=bias_rows[:], op=ALU.add
+                    out=c_planes[(rnd // PACK, b)][:, rnd % PACK, :],
+                    in0=mixed[(rnd, b)][:],
+                    in1=bias_rows[rnd][:],
+                    op=ALU.add,
                 )
 
-        def quantise_c(sweep, g, c_planes):
-            cols = slice(sweep * N_TILE, (sweep + 1) * N_TILE)
+        def regroup_c(rnd):
+            if not (0 <= rnd < ROUNDS and rnd % PACK == PACK - 1):
+                return
             copies = (nc.vector.tensor_copy, nc.scalar.copy)
             for b in range(B):
-                c_grouped = grouped_pool.tile([P, N_TILE, PACK], BF16, tag="grouped", align_bytes=64)
-                regroup(copies[b], c_grouped[:], c_planes[b][:])
+                c_grouped[(rnd, b)] = grouped_pool.tile(
+                    [P, N_TILE, PACK], BF16, name="c_grouped", tag="grouped", align_bytes=64
+                )
+                regroup(copies[b], c_grouped[(rnd, b)][:], c_planes[(rnd // PACK, b)][:])
+
+        def quantise_c(rnd):
+            if not (0 <= rnd < ROUNDS and rnd % PACK == PACK - 1):
+                return
+            sweep, pair = divmod(rnd, PAIRS)
+            cols = slice(sweep * N_TILE, (sweep + 1) * N_TILE)
+            for b in range(B):
                 nc.vector.quantize_mx(
-                    out=c_words[:, b, g, cols].bitcast(FP8X4),
-                    scales=c_scales[:, b, g, cols],
-                    in_=c_grouped[:].rearrange("q s j -> q (s j)"),
+                    out=c_words[:, b, pair // PACK, cols].bitcast(FP8X4),
+                    scales=c_scales[:, b, pair // PACK, cols],
+                    in_=c_grouped[(rnd, b)][:].rearrange("q s j -> q (s j)"),
                 )
 
-        def project(b, sweep, n_half):
+        def patch_of(item):
+            sweep, rest = divmod(item // BLOCKS, B * 2)
+            return sweep, rest // 2, rest % 2
+
+        def project(item):
+            if not 0 <= item < ITEMS:
+                return
+            sweep, b, n_half = patch_of(item)
+            n_block = n_half * BLOCKS + item % BLOCKS
+            cols = slice(n_block * P, (n_block + 1) * P)
             steps = slice(sweep * N_TILE, (sweep + 1) * N_TILE)
-            y_turned = turned_pool.tile([P, BLOCKS, N_TILE], F32)
-            for i in range(BLOCKS):
-                n_block = n_half * BLOCKS + i
-                cols = slice(n_block * P, (n_block + 1) * P)
-                projected = psum_out.tile([P, N_TILE], F32)
-                for g in range(2):
-                    nc.tensor.matmul_mx(
-                        out=projected[:],
-                        lhsT=w_words[:, g, cols].bitcast(FP8X4),
-                        lhsT_scale=w_scales[:, g, cols],
-                        rhs=c_words[:, b, g, steps].bitcast(FP8X4),
-                        rhs_scale=c_scales[:, b, g, steps],
-                        start=(g == 0),
-                        stop=(g == 1),
-                    )
-                nc.scalar.activation(
-                    out=y_turned[:, i, :],
-                    in_=projected[:],
-                    func=ACT.Identity,
-                    bias=out_b_column[:, n_block : n_block + 1],
+            projected[item] = psum_out.tile([P, N_TILE], F32, name="projected")
+            for g in range(E // K_PASS):
+                nc.tensor.matmul_mx(
+                    out=projected[item][:],
+                    lhsT=w_words[:, g, cols].bitcast(FP8X4),
+                    lhsT_scale=w_scales[:, g, cols],
+                    rhs=c_words[:, b, g, steps].bitcast(FP8X4),
+                    rhs_scale=c_scales[:, b, g, steps],
+                    start=(g == 0),
+                    stop=(g == E // K_PASS - 1),
                 )
-            n_cols = slice(n_half * N_TILE, (n_half + 1) * N_TILE)
-            for block in range(BLOCKS):
-                rows = slice(sweep * N_TILE + block * P, sweep * N_TILE + (block + 1) * P)
-                x_raw = x_pool.tile([P, N_TILE], BF16)
-                nc.sync.dma_start(out=x_raw[:], in_=x[b, rows, n_cols])
-                turned_back = psum_back.tile([P, N_TILE], F32)
-                for i in range(BLOCKS):
-                    nc.tensor.transpose(
-                        out=turned_back[:, i * P : (i + 1) * P],
-                        in_=y_turned[:, i, block * P : (block + 1) * P],
-                        identity=identity_f32[:],
-                    )
-                y = y_pool.tile([P, N_TILE], F32)
-                nc.vector.tensor_tensor(out=y[:], in0=turned_back[:], in1=x_raw[:], op=ALU.add)
-                nc.sync.dma_start(out=out[b, rows, n_cols], in_=y[:])
 
-        for sweep in range(SWEEPS):
-            c_planes = []
-            for pair in range(PAIRS):
-                if sweep == 0:
-                    quantise_p(pair)
-                    if pair < E // K_PASS:
-                        quantise_out_w(pair)
-                elif pair % 2 == 0:
-                    project(pair // PACK, 0, (pair // 2) % 2)
-                if pair % PACK == 0:
-                    c_planes = [
-                        c_pool.tile([P, PACK, N_TILE], BF16, name="c_planes") for b in range(B)
-                    ]
-                mix(sweep, pair, c_planes)
-                if pair % PACK == PACK - 1:
-                    quantise_c(sweep, pair // PACK, c_planes)
-        for b in range(B):
-            for n_half in range(E // N_TILE):
-                project(b, 1, n_half)
+        def add_out_b(item):
+            if not 0 <= item < ITEMS:
+                return
+            patch, i = divmod(item, BLOCKS)
+            n_block = patch_of(item)[2] * BLOCKS + i
+            if i == 0:
+                y_turned[patch] = turned_pool.tile([P, BLOCKS, N_TILE], F32, name="y_turned")
+            nc.scalar.activation(
+                out=y_turned[patch][:, i, :],
+                in_=projected[item][:],
+                func=ACT.Identity,
+                bias=out_b_column[:, n_block : n_block + 1],
+            )
+
+        def rows_and_cols(item):
+            sweep, b, n_half = patch_of(item)
+            first = sweep * N_TILE + (item % BLOCKS) * P
+            return b, slice(first, first + P), slice(n_half * N_TILE, (n_half + 1) * N_TILE)
+
+        def load_x(item):
+            if not 0 <= item < ITEMS:
+                return
+            b, rows, cols = rows_and_cols(item)
+            x_raw[item] = x_pool.tile([P, N_TILE], BF16, name="x_raw")
+            nc.sync.dma_start(out=x_raw[item][:], in_=x[b, rows, cols])
+
+        def turn_back(item):
+            if not 0 <= item < ITEMS:
+                return
+            patch, block = divmod(item, BLOCKS)
+            turned_back[item] = psum_back.tile([P, N_TILE], F32, name="turned_back")
+            for i in range(BLOCKS):
+                nc.tensor.transpose(
+                    out=turned_back[item][:, i * P : (i + 1) * P],
+                    in_=y_turned[patch][:, i, block * P : (block + 1) * P],
+                    identity=identity_f32[:],
+                )
+
+        def add_x_and_store(item):
+            if not 0 <= item < ITEMS:
+                return
+            b, rows, cols = rows_and_cols(item)
+            y = y_pool.tile([P, N_TILE], F32)
+            nc.vector.tensor_tensor(out=y[:], in0=turned_back[item][:], in1=x_raw[item][:], op=ALU.add)
+            nc.sync.dma_start(out=out[b, rows, cols], in_=y[:])
+
+        with tc.manual_schedule():
+            for step in range(-4, UNITS + FIRST_ITEM + 7):
+                rnd, second = divmod(step, 2)
+                item = step - FIRST_ITEM
+                if not second:
+                    load_p(rnd + 2)
+                    load_bias(rnd + 1)
+                load_out_w(step + 4)
+                load_x(item - 3)
+                project(item)
+                add_out_b(item - 1)
+                turn_back(item - 5)
+                spread_right(step + 2)
+                write_chunks(step + 1)
+                quantise_out_w(step + 2)
+                regroup_m(step)
+                if not second:
+                    regroup_p(rnd + 1)
+                    add_bias(rnd - 1)
+                    regroup_c(rnd - 1)
+                add_x_and_store(item - 6)
+                quantise_m(step)
+                if second:
+                    quantise_p(rnd + 1)
+                    quantise_c(rnd - 1)
+                    multiply(rnd)

from contextlib import ExitStack

import concourse.mybir as mybir
from concourse.masks import make_identity

F32 = mybir.dt.float32
BF16 = mybir.dt.bfloat16
I32 = mybir.dt.int32
U32 = mybir.dt.uint32
U8 = mybir.dt.uint8
FP8X4 = mybir.dt.float8_e4m3fn_x4
ALU = mybir.AluOpType
ACT = mybir.ActivationFunctionType

P = 128
PACK = 4
K_PASS = P * PACK
B, H, T, HD = 2, 16, 1024, 64
E = H * HD
HALF_H = H // 2
CHUNKS = T // P
PAIRS = H // 2
N_TILE = 512
SWEEPS = T // N_TILE
BLOCKS = N_TILE // P
UNITS = SWEEPS * H
ROUNDS = SWEEPS * PAIRS
ITEMS = SWEEPS * B * (E // N_TILE) * BLOCKS
FIRST_ITEM = H + 2

FLOPS = 2 * B * H * HD * (K_PASS * N_TILE + T * N_TILE) + 2 * B * T * E * E


def regroup(engine_copy, grouped, planes):
    engine_copy(
        out=grouped.rearrange("q (c i) j -> q c j i", i=4),
        in_=planes.rearrange("q j (c i) -> q c j i", i=4),
    )


def tile_mixerblock_pa_kernel(tc, p, mix_w, mix_b, decay, out_w, out_b, x, out):
    nc = tc.nc
    with ExitStack() as stack:
        def pool(name, bufs):
            return stack.enter_context(tc.tile_pool(name=name, bufs=bufs))

        const = pool("const", 1)
        grouped_pool = pool("grouped", 4)
        m_pool = pool("m_words", 6)
        p_pool = pool("p_stage", 2)
        bias_pool = pool("bias_rows", 3)
        c_pool = pool("c_planes", 4)
        w_pool = pool("w_stage", 2)
        x_pool = pool("x_stage", 5)
        turned_pool = pool("y_turned", 3)
        y_pool = pool("y_stage", 3)
        psum_right = stack.enter_context(tc.psum_pool(name="psum_right", bufs=2))
        psum_mix = stack.enter_context(tc.psum_pool(name="psum_mix", bufs=2))
        psum_out = stack.enter_context(tc.psum_pool(name="psum_out", bufs=2))
        psum_back = stack.enter_context(tc.psum_pool(name="psum_back", bufs=2))

        column_int = const.tile([P, P], I32)
        nc.gpsimd.iota(column_int[:], pattern=[[1, P]], base=0, channel_multiplier=0)
        column = const.tile([P, P], F32)
        nc.vector.tensor_copy(out=column[:], in_=column_int[:])
        t_int = const.tile([P, CHUNKS], I32)
        nc.gpsimd.iota(t_int[:], pattern=[[P, CHUNKS]], base=0, channel_multiplier=1)
        t_index = const.tile([P, CHUNKS], F32)
        nc.vector.tensor_copy(out=t_index[:], in_=t_int[:])
        triangle = const.tile([P, P], BF16)
        nc.vector.tensor_scalar(
            out=triangle[:], in0=column[:], scalar1=t_index[:, 0:1], scalar2=None, op0=ALU.is_ge
        )
        identity_bf16 = const.tile([P, P], BF16)
        make_identity(nc, identity_bf16[:])
        identity_f32 = const.tile([P, P], F32)
        make_identity(nc, identity_f32[:])

        decay_rows = const.tile([P, H], BF16)
        nc.sync.dma_start(out=decay_rows[:], in_=decay.partition_broadcast(P))
        d_clipped = const.tile([P, H], F32)
        nc.vector.tensor_scalar(
            out=d_clipped[:], in0=decay_rows[:], scalar1=0.9, scalar2=1.0, op0=ALU.max, op1=ALU.min
        )
        log_d = const.tile([P, H], F32)
        nc.scalar.activation(out=log_d[:], in_=d_clipped[:], func=ACT.Ln)

        w_rows = const.tile([P, P], BF16)
        nc.sync.dma_start(out=w_rows[:], in_=mix_w.rearrange("h (a q) -> (h a) q", q=P))
        w_turned = psum_right.tile([P, P], BF16, tag="right")
        nc.tensor.transpose(out=w_turned[:], in_=w_rows[:], identity=identity_bf16[:])
        w_by_t = const.tile([P, H, CHUNKS], F32)
        nc.vector.tensor_copy(out=w_by_t[:].rearrange("q h a -> q (h a)"), in_=w_turned[:])

        exponent = const.tile([P, H, CHUNKS], F32)
        nc.vector.tensor_tensor(
            out=exponent[:],
            in0=t_index[:].unsqueeze(1).to_broadcast([P, H, CHUNKS]),
            in1=log_d[:].unsqueeze(2).to_broadcast([P, H, CHUNKS]),
            op=ALU.mult,
        )
        right = const.tile([P, H, CHUNKS], F32)
        nc.scalar.activation(out=right[:], in_=exponent[:], func=ACT.Exp, scale=0.5)
        left = const.tile([P, H, CHUNKS], F32)
        nc.scalar.activation(out=left[:], in_=exponent[:], func=ACT.Exp, scale=-0.5)
        nc.vector.tensor_tensor(
            out=right[:, 0:HALF_H, :], in0=right[:, 0:HALF_H, :], in1=w_by_t[:, 0:HALF_H, :], op=ALU.mult
        )
        nc.vector.tensor_tensor(
            out=left[:, HALF_H:H, :], in0=left[:, HALF_H:H, :], in1=w_by_t[:, HALF_H:H, :], op=ALU.mult
        )

        out_b_rows = const.tile([P, P], BF16)
        nc.vector.memset(out_b_rows[:], 0.0)
        nc.sync.dma_start(out=out_b_rows[0 : E // P, :], in_=out_b.rearrange("(i q) -> i q", q=P))
        out_b_turned = psum_right.tile([P, P], BF16, tag="right")
        nc.tensor.transpose(out=out_b_turned[:], in_=out_b_rows[:], identity=identity_bf16[:])
        out_b_column = const.tile([P, E // P], F32)
        nc.vector.tensor_copy(out=out_b_column[:], in_=out_b_turned[:, 0 : E // P])

        full_piece, diag_piece, diag_blocks = [], [], []
        for odd in range(2):
            full = const.tile([P, PACK, N_TILE], BF16, name="full_piece%d" % odd)
            flat = const.tile([P, PACK * (N_TILE + P)], BF16, name="diag_piece%d" % odd)
            full_piece.append(full[:])
            diag_piece.append(flat[:, 0 : PACK * N_TILE].rearrange("q (j s) -> q j s", j=PACK))
            diag_blocks.append(flat[:].rearrange("q (j s) -> q j s", j=PACK)[:, :, 0:P])
            for j in range(1, PACK):
                nc.vector.memset(diag_piece[odd][:, j, 0 : P * j], 0.0)

        p_words = const.tile([P, PAIRS, B * 2, 3 * HD], U32, align_bytes=64)
        p_scales = const.tile([P, PAIRS, B * 2, 3 * HD], U8, align_bytes=64)
        nc.vector.memset(p_words[:, :, :, HD : 2 * HD].bitcast(I32), 0)
        nc.vector.memset(p_scales[:, :, :, HD : 2 * HD].bitcast(I32), 0)

        c_words = const.tile([P, B, 2, T], U32, align_bytes=64)
        c_scales = const.tile([P, B, 2, T], U8, align_bytes=64)
        w_words = const.tile([P, 2, E], U32, align_bytes=64)
        w_scales = const.tile([P, 2, E], U8, align_bytes=64)

        p_raw, p_grouped, w_raw, bias_rows, right_rows = {}, {}, {}, {}, {}
        m_grouped, m_words, m_scales, mixed, c_planes, c_grouped = {}, {}, {}, {}, {}, {}
        projected, y_turned, turned_back, x_raw = {}, {}, {}, {}

        def load_p(pair):
            if not 0 <= pair < PAIRS:
                return
            p_raw[pair] = p_pool.tile([P, B, 2 * CHUNKS, HD], BF16, name="p_raw")
            for b in range(B):
                nc.sync.dma_start(
                    out=p_raw[pair][:, b, :, :],
                    in_=p[b, 2 * pair : 2 * pair + 2, :, :].rearrange("h (a q) f -> q (h a) f", q=P),
                )

        def regroup_p(pair):
            if not 0 <= pair < PAIRS:
                return
            p_grouped[pair] = p_pool.tile(
                [P, B, 2 * 2, HD, PACK], BF16, name="p_grouped", align_bytes=64
            )
            for b in range(B):
                nc.scalar.copy(
                    out=p_grouped[pair][:, b, :, :, :],
                    in_=p_raw[pair][:, b, :, :].rearrange("q (g j) f -> q g f j", j=PACK),
                )

        def quantise_p(pair):
            if not 0 <= pair < PAIRS:
                return
            for b in range(B):
                for odd in range(2):
                    for c in range(2):
                        cols = slice(2 * HD * odd, 2 * HD * odd + HD)
                        nc.vector.quantize_mx(
                            out=p_words[:, pair, 2 * b + c, cols].bitcast(FP8X4),
                            scales=p_scales[:, pair, 2 * b + c, cols],
                            in_=p_grouped[pair][:, b, 2 * odd + c, :, :].rearrange("q f j -> q (f j)"),
                        )

        def load_out_w(g):
            if not 0 <= g < E // K_PASS:
                return
            w_raw[g] = w_pool.tile([P, PACK, E], BF16, name="w_raw")
            nc.sync.dma_start(
                out=w_raw[g][:],
                in_=out_w[g * K_PASS : (g + 1) * K_PASS, :].rearrange("(j q) n -> q j n", q=P),
            )

        def quantise_out_w(g):
            if not 0 <= g < E // K_PASS:
                return
            w_grouped = w_pool.tile([P, E, PACK], BF16, align_bytes=64)
            regroup(nc.vector.tensor_copy, w_grouped[:], w_raw[g][:])
            nc.vector.quantize_mx(
                out=w_words[:, g, :].bitcast(FP8X4),
                scales=w_scales[:, g, :],
                in_=w_grouped[:].rearrange("q n j -> q (n j)"),
            )

        def spread_right(unit):
            if not 0 <= unit < UNITS:
                return
            sweep, h = divmod(unit, H)
            right_rows[unit] = psum_right.tile([P, N_TILE], F32, name="right_rows", tag="right")
            for i in range(BLOCKS):
                a = sweep * BLOCKS + i
                nc.tensor.transpose(
                    out=right_rows[unit][:, i * P : (i + 1) * P],
                    in_=right[:, h, a : a + 1].to_broadcast([P, P]),
                    identity=identity_f32[:],
                )

        def planes_of(unit, c):
            sweep, h = divmod(unit, H)
            return diag_piece[h % 2] if c == sweep else full_piece[h % 2]

        def write_chunks(unit):
            if not 0 <= unit < UNITS:
                return
            sweep, h = divmod(unit, H)
            for c in range(sweep + 1):
                for j in range(PACK):
                    first = P * j if c == sweep else 0
                    nc.scalar.activation(
                        out=planes_of(unit, c)[:, j, first:N_TILE],
                        in_=right_rows[unit][:, first:N_TILE],
                        func=ACT.Copy,
                        scale=left[:, h, PACK * c + j : PACK * c + j + 1],
                    )

        def regroup_m(unit):
            if not 0 <= unit < UNITS:
                return
            sweep, h = divmod(unit, H)
            nc.vector.tensor_tensor(
                out=diag_blocks[h % 2],
                in0=diag_blocks[h % 2],
                in1=triangle[:].unsqueeze(1).to_broadcast([P, PACK, P]),
                op=ALU.mult,
            )
            for c in range(sweep + 1):
                m_grouped[(unit, c)] = grouped_pool.tile(
                    [P, N_TILE, PACK], BF16, name="m_grouped", tag="grouped", align_bytes=64
                )
                regroup(nc.vector.tensor_copy, m_grouped[(unit, c)][:], planes_of(unit, c))

        def quantise_m(unit):
            if not 0 <= unit < UNITS:
                return
            for c in range(unit // H + 1):
                m_words[(unit, c)] = m_pool.tile([P, N_TILE], U32, name="m_words", align_bytes=64)
                m_scales[(unit, c)] = m_pool.tile([P, N_TILE], U8, name="m_scales", align_bytes=64)
                nc.vector.quantize_mx(
                    out=m_words[(unit, c)][:].bitcast(FP8X4),
                    scales=m_scales[(unit, c)][:],
                    in_=m_grouped[(unit, c)][:].rearrange("q s j -> q (s j)"),
                )

        def load_bias(rnd):
            if not 0 <= rnd < ROUNDS:
                return
            sweep, pair = divmod(rnd, PAIRS)
            bias_rows[rnd] = bias_pool.tile([P, N_TILE], BF16, name="bias_rows")
            for odd in range(2):
                nc.sync.dma_start(
                    out=bias_rows[rnd][HD * odd : HD * (odd + 1), :],
                    in_=mix_b[2 * pair + odd, sweep * N_TILE : (sweep + 1) * N_TILE].partition_broadcast(HD),
                )

        def multiply(rnd):
            if not 0 <= rnd < ROUNDS:
                return
            sweep, pair = divmod(rnd, PAIRS)
            passes = [(odd, c) for odd in range(2) for c in range(sweep + 1)]
            for b in range(B):
                mixed[(rnd, b)] = psum_mix.tile([P, N_TILE], F32, name="mixed")
                for i, (odd, c) in enumerate(passes):
                    cols = slice(HD * odd, HD * odd + P)
                    unit = 2 * rnd + odd
                    nc.tensor.matmul_mx(
                        out=mixed[(rnd, b)][:],
                        lhsT=p_words[:, pair, 2 * b + c, cols].bitcast(FP8X4),
                        lhsT_scale=p_scales[:, pair, 2 * b + c, cols],
                        rhs=m_words[(unit, c)][:].bitcast(FP8X4),
                        rhs_scale=m_scales[(unit, c)][:],
                        start=(i == 0),
                        stop=(i == len(passes) - 1),
                    )

        def add_bias(rnd):
            if not 0 <= rnd < ROUNDS:
                return
            for b in range(B):
                if rnd % PACK == 0:
                    c_planes[(rnd // PACK, b)] = c_pool.tile([P, PACK, N_TILE], BF16, name="c_planes")
                nc.vector.tensor_tensor(
                    out=c_planes[(rnd // PACK, b)][:, rnd % PACK, :],
                    in0=mixed[(rnd, b)][:],
                    in1=bias_rows[rnd][:],
                    op=ALU.add,
                )

        def regroup_c(rnd):
            if not (0 <= rnd < ROUNDS and rnd % PACK == PACK - 1):
                return
            copies = (nc.vector.tensor_copy, nc.scalar.copy)
            for b in range(B):
                c_grouped[(rnd, b)] = grouped_pool.tile(
                    [P, N_TILE, PACK], BF16, name="c_grouped", tag="grouped", align_bytes=64
                )
                regroup(copies[b], c_grouped[(rnd, b)][:], c_planes[(rnd // PACK, b)][:])

        def quantise_c(rnd):
            if not (0 <= rnd < ROUNDS and rnd % PACK == PACK - 1):
                return
            sweep, pair = divmod(rnd, PAIRS)
            cols = slice(sweep * N_TILE, (sweep + 1) * N_TILE)
            for b in range(B):
                nc.vector.quantize_mx(
                    out=c_words[:, b, pair // PACK, cols].bitcast(FP8X4),
                    scales=c_scales[:, b, pair // PACK, cols],
                    in_=c_grouped[(rnd, b)][:].rearrange("q s j -> q (s j)"),
                )

        def patch_of(item):
            sweep, rest = divmod(item // BLOCKS, B * 2)
            return sweep, rest // 2, rest % 2

        def project(item):
            if not 0 <= item < ITEMS:
                return
            sweep, b, n_half = patch_of(item)
            n_block = n_half * BLOCKS + item % BLOCKS
            cols = slice(n_block * P, (n_block + 1) * P)
            steps = slice(sweep * N_TILE, (sweep + 1) * N_TILE)
            projected[item] = psum_out.tile([P, N_TILE], F32, name="projected")
            for g in range(E // K_PASS):
                nc.tensor.matmul_mx(
                    out=projected[item][:],
                    lhsT=w_words[:, g, cols].bitcast(FP8X4),
                    lhsT_scale=w_scales[:, g, cols],
                    rhs=c_words[:, b, g, steps].bitcast(FP8X4),
                    rhs_scale=c_scales[:, b, g, steps],
                    start=(g == 0),
                    stop=(g == E // K_PASS - 1),
                )

        def add_out_b(item):
            if not 0 <= item < ITEMS:
                return
            patch, i = divmod(item, BLOCKS)
            n_block = patch_of(item)[2] * BLOCKS + i
            if i == 0:
                y_turned[patch] = turned_pool.tile([P, BLOCKS, N_TILE], F32, name="y_turned")
            nc.scalar.activation(
                out=y_turned[patch][:, i, :],
                in_=projected[item][:],
                func=ACT.Identity,
                bias=out_b_column[:, n_block : n_block + 1],
            )

        def rows_and_cols(item):
            sweep, b, n_half = patch_of(item)
            first = sweep * N_TILE + (item % BLOCKS) * P
            return b, slice(first, first + P), slice(n_half * N_TILE, (n_half + 1) * N_TILE)

        def load_x(item):
            if not 0 <= item < ITEMS:
                return
            b, rows, cols = rows_and_cols(item)
            x_raw[item] = x_pool.tile([P, N_TILE], BF16, name="x_raw")
            nc.sync.dma_start(out=x_raw[item][:], in_=x[b, rows, cols])

        def turn_back(item):
            if not 0 <= item < ITEMS:
                return
            patch, block = divmod(item, BLOCKS)
            turned_back[item] = psum_back.tile([P, N_TILE], F32, name="turned_back")
            for i in range(BLOCKS):
                nc.tensor.transpose(
                    out=turned_back[item][:, i * P : (i + 1) * P],
                    in_=y_turned[patch][:, i, block * P : (block + 1) * P],
                    identity=identity_f32[:],
                )

        def add_x_and_store(item):
            if not 0 <= item < ITEMS:
                return
            b, rows, cols = rows_and_cols(item)
            y = y_pool.tile([P, N_TILE], F32)
            nc.vector.tensor_tensor(out=y[:], in0=turned_back[item][:], in1=x_raw[item][:], op=ALU.add)
            nc.sync.dma_start(out=out[b, rows, cols], in_=y[:])

        with tc.manual_schedule():
            for step in range(-4, UNITS + FIRST_ITEM + 7):
                rnd, second = divmod(step, 2)
                item = step - FIRST_ITEM
                if not second:
                    load_p(rnd + 2)
                    load_bias(rnd + 1)
                load_out_w(step + 4)
                load_x(item - 3)
                project(item)
                add_out_b(item - 1)
                turn_back(item - 5)
                spread_right(step + 2)
                write_chunks(step + 1)
                quantise_out_w(step + 2)
                regroup_m(step)
                if not second:
                    regroup_p(rnd + 1)
                    add_bias(rnd - 1)
                    regroup_c(rnd - 1)
                add_x_and_store(item - 6)
                quantise_m(step)
                if second:
                    quantise_p(rnd + 1)
                    quantise_c(rnd - 1)
                    multiply(rnd)
